import numpy as np
import ml_dtypes


def mxq(x, axis, fmt="e4m3"):
    dtype, down = {"e4m3": (ml_dtypes.float8_e4m3fn, 7), "e5m2": (ml_dtypes.float8_e5m2, 14)}[fmt]
    v = np.moveaxis(np.asarray(x, np.float32).astype(ml_dtypes.bfloat16).astype(np.float64), axis, -1)
    blocks = v.reshape(v.shape[:-1] + (-1, 32))
    amax = np.abs(blocks).max(-1, keepdims=True)
    byte = np.maximum(np.where(amax > 0, np.frexp(amax)[1] - 1 + 127, 0) - down, 1)
    scale = np.exp2(byte - 127.0)
    codes = (blocks / scale).astype(np.float32).astype(dtype).astype(np.float64)
    return np.moveaxis((codes * scale).reshape(v.shape), -1, axis)


WIDE = False


def mx_kscale(k):
    if not WIDE:
        return np.ones(k)
    levels = np.array([10, -10, 5, -5, 0])
    a = np.random.permutation(np.resize(levels, k // 512 * 4)).reshape(k // 512, 4)
    idx = np.arange(k)
    return np.exp2(a[idx // 512, idx % 128 // 32])


BF16 = ml_dtypes.bfloat16


def bf(x):
    return np.asarray(x, np.float32).astype(BF16)


def f64(x):
    return np.asarray(x).astype(np.float64)


E2M1 = np.array([0.0, 0.5, 1.0, 1.5, 2.0, 3.0, 4.0, 6.0, -0.0, -0.5, -1.0, -1.5, -2.0, -3.0, -4.0, -6.0])


def pack_weight(w, fmt):
    k, n = w.shape
    w = f64(bf(w)).reshape(k // 32, 32, n)
    amax = np.abs(w).max(1)
    if fmt == "e4m3":
        byte = np.frexp(amax)[1] - 1 + 127 - 7
    else:
        mant, ex = np.frexp(amax / 6.0)
        byte = np.where(mant > 0.5, ex, ex - 1) + 127
    byte = np.clip(np.where(amax > 0, byte, 1), 1, 254)
    scaled = (w * np.exp2(127.0 - byte)[:, None, :]).reshape(k, n).astype(np.float32)
    by_word = np.ascontiguousarray(scaled.reshape(k // 512, 128, 4, n).transpose(0, 1, 3, 2))
    if fmt == "e4m3":
        words = by_word.astype(ml_dtypes.float8_e4m3fn).view(np.uint8)
    else:
        c = by_word.astype(ml_dtypes.float4_e2m1fn).view(np.uint8) & 0xF
        words = c[..., 0::2] | (c[..., 1::2] << 4)
    return np.ascontiguousarray(words), np.ascontiguousarray(byte.astype(np.uint8).reshape(k // 512, 16, n))


def unpack_weight(words, scales, fmt):
    g, p, n, _ = words.shape
    if fmt == "e4m3":
        vals = np.ascontiguousarray(words).view(ml_dtypes.float8_e4m3fn).astype(np.float64)
    else:
        nib = np.empty((g, p, n, 4), np.uint8)
        nib[..., 0::2] = words & 0xF
        nib[..., 1::2] = words >> 4
        vals = E2M1[nib]
    vals = vals * np.repeat(np.exp2(scales.astype(np.float64) - 127.0), 8, axis=1)[..., None]
    return vals.transpose(0, 1, 3, 2).reshape(g * 512, n)


B, IN, HID = 1024, 512, 512
FMT = "e4m3"


def sigmoid(v):
    return 1.0 / (1.0 + np.exp(-v))


def lin(xq, words, scales):
    return xq @ unpack_weight(words, scales, FMT)


def setup_inputs():
    s, p = mx_kscale(IN), mx_kscale(HID)
    inputs = bf(np.random.standard_normal((B, IN)) * s)
    state = bf(np.random.standard_normal((B, HID)))
    parent_state = bf(np.random.standard_normal((B, HID)) * p)
    c = bf(np.tanh(np.random.standard_normal((B, HID))))
    w_a_w_words, w_a_w_scales = pack_weight((np.random.standard_normal((HID, IN)) * 0.6 / np.sqrt(IN) / s).T, FMT)
    w_a_b = bf(np.random.standard_normal(HID) * 0.5)
    u_a_w_words, u_a_w_scales = pack_weight((np.random.standard_normal((HID, HID)) * 0.6 / np.sqrt(HID)).T, FMT)
    p_a_w_words, p_a_w_scales = pack_weight((np.random.standard_normal((HID, HID)) * 0.6 / np.sqrt(HID) / p).T, FMT)
    return {"inputs": inputs,
            "state": state,
            "parent_state": parent_state,
            "c": c,
            "w_a_w_words": w_a_w_words,
            "w_a_w_scales": w_a_w_scales,
            "w_a_b": w_a_b,
            "u_a_w_words": u_a_w_words,
            "u_a_w_scales": u_a_w_scales,
            "p_a_w_words": p_a_w_words,
            "p_a_w_scales": p_a_w_scales}


def reference(inputs, state, parent_state, c, w_a_w_words, w_a_w_scales, w_a_b, u_a_w_words, u_a_w_scales, p_a_w_words, p_a_w_scales):
    st = f64(state)
    att = sigmoid(lin(mxq(f64(inputs), 1, "e4m3"), w_a_w_words, w_a_w_scales) + f64(w_a_b) + lin(mxq(st, 1, "e4m3"), u_a_w_words, u_a_w_scales) + lin(mxq(f64(parent_state), 1, "e4m3"), p_a_w_words, p_a_w_scales))
    return att * f64(c) + (1.0 - att) * st

@@ -1,0 +1,188 @@
+from contextlib import ExitStack
+
+import concourse.masks as masks
+import concourse.mybir as mybir
+
+F32 = mybir.dt.float32
+BF16 = mybir.dt.bfloat16
+I32 = mybir.dt.int32
+U32 = mybir.dt.uint32
+U8 = mybir.dt.uint8
+FP8X4 = mybir.dt.float8_e4m3fn_x4
+ADD = mybir.AluOpType.add
+SUB = mybir.AluOpType.subtract
+MULT = mybir.AluOpType.mult
+SIGMOID = mybir.ActivationFunctionType.Sigmoid
+
+P = 128
+PACK = 4
+BATCH = 1024
+K = 512
+HID = 512
+OPERANDS = 3
+STATE = 1
+TILES = BATCH // P
+CHUNK = 2
+CHUNKS = TILES // CHUNK
+CHUNK_ROWS = CHUNK * P
+SLICES = HID // P
+BANK_SLICES = 2
+QUADRANT = 32
+LIVE = 4
+
+FLOPS = 2 * BATCH * OPERANDS * K * HID
+
+
+def tile_parentgru_pb_kernel(
+    tc,
+    inputs,
+    state,
+    parent_state,
+    c,
+    w_a_w_words,
+    w_a_w_scales,
+    w_a_b,
+    u_a_w_words,
+    u_a_w_scales,
+    p_a_w_words,
+    p_a_w_scales,
+    out,
+):
+    nc = tc.nc
+    activations = (inputs, state, parent_state)
+    weight_words = (w_a_w_words, u_a_w_words, p_a_w_words)
+    weight_scales = (w_a_w_scales, u_a_w_scales, p_a_w_scales)
+
+    with ExitStack() as ctx:
+        keep = ctx.enter_context(tc.tile_pool(name="keep", bufs=1))
+        work = ctx.enter_context(tc.tile_pool(name="work", bufs=3))
+        psum_x = ctx.enter_context(tc.psum_pool(name="psum_x", bufs=3))
+        psum_z = ctx.enter_context(tc.psum_pool(name="psum_z", bufs=2))
+        psum_a = ctx.enter_context(tc.psum_pool(name="psum_a", bufs=2))
+        ctx.enter_context(tc.manual_schedule())
+
+        def by_tile(dram):
+            return dram.rearrange("(p j) f -> p j f", j=TILES)
+
+        x_sb = [keep.tile([P, TILES, K], BF16, name="x_sb%d" % o) for o in range(OPERANDS)]
+        c_sb = keep.tile([P, TILES, HID], BF16)
+        w_codes = keep.tile([P, OPERANDS, HID * PACK], U8, align_bytes=64)
+        w_planes = keep.tile([P, OPERANDS, HID], U8, align_bytes=64)
+        x_codes = keep.tile([P, OPERANDS, BATCH], U32, align_bytes=64)
+        x_planes = keep.tile([P, OPERANDS, BATCH], U8, align_bytes=64)
+        diff = keep.tile([P, TILES, HID], F32)
+        out_sb = keep.tile([P, TILES, HID], F32)
+        ident = keep.tile([P, P], F32)
+        bias_rows = keep.tile([P, P], BF16)
+        bias_rows_f32 = keep.tile([P, P], F32)
+        bias_cols = keep.tile([P, SLICES], F32)
+        warm = keep.tile([P, 1], F32)
+
+        nc.vector.memset(w_planes[:].bitcast(I32), 0)
+        nc.vector.memset(bias_rows[:], 0.0)
+        nc.vector.memset(warm[:], 0.0)
+        masks.make_identity(nc, ident[:])
+        nc.scalar.activation(out=warm[:], in_=warm[:], func=SIGMOID)
+
+        def load_chunk(ch):
+            tiles = slice(ch * CHUNK, (ch + 1) * CHUNK)
+            for o in range(OPERANDS):
+                nc.sync.dma_start(out=x_sb[o][:, tiles, :], in_=by_tile(activations[o])[:, tiles, :])
+            nc.gpsimd.dma_start(out=c_sb[:, tiles, :], in_=by_tile(c)[:, tiles, :])
+
+        load_chunk(0)
+        nc.sync.dma_start(out=bias_rows[0:SLICES, :], in_=w_a_b.rearrange("(s m) -> s m", m=P))
+        for o in range(OPERANDS):
+            for quad in range(P // QUADRANT):
+                nc.sync.dma_start(
+                    out=w_planes[quad * QUADRANT : quad * QUADRANT + LIVE, o, :].bitcast(I32),
+                    in_=weight_scales[o].bitcast(I32)[0, quad * LIVE : (quad + 1) * LIVE, :],
+                )
+            nc.sync.dma_start(
+                out=w_codes[:, o, :].bitcast(I32),
+                in_=weight_words[o][0].rearrange("p n t -> p (n t)").bitcast(I32),
+            )
+        for ch in range(1, CHUNKS):
+            load_chunk(ch)
+
+        def quantise(ch, o):
+            cols = slice(ch * CHUNK_ROWS, (ch + 1) * CHUNK_ROWS)
+            words = x_sb[o][:].bitcast(F32).rearrange("r j (p u) -> r j u p", u=2)
+            xt = psum_x.tile([P, CHUNK, 2, P], F32, tag="xt")
+            for j in range(CHUNK):
+                for u in range(2):
+                    nc.tensor.transpose(xt[:, j, u, :], words[:, ch * CHUNK + j, u, :], ident[:])
+            grouped = work.tile([P, CHUNK_ROWS * PACK], BF16, align_bytes=64)
+            nc.scalar.copy(
+                out=grouped[:].bitcast(F32).rearrange("p (j r u) -> p j r u", j=CHUNK, u=2),
+                in_=xt[:].rearrange("p j u r -> p j r u"),
+            )
+            nc.vector.quantize_mx(
+                out=x_codes[:, o, cols].bitcast(FP8X4),
+                scales=x_planes[:, o, cols],
+                in_=grouped[:],
+            )
+
+        def bias_to_partitions():
+            nc.vector.tensor_copy(out=bias_rows_f32[:], in_=bias_rows[:])
+            bias_t = psum_x.tile([P, P], F32, tag="xt")
+            nc.tensor.transpose(bias_t[:], bias_rows_f32[:], ident[:])
+            nc.vector.tensor_copy(out=bias_cols[:], in_=bias_t[:, 0:SLICES])
+
+        def gate(ch, att_t, bank):
+            cols = slice(ch * CHUNK_ROWS, (ch + 1) * CHUNK_ROWS)
+            z = psum_z.tile([P, BANK_SLICES, CHUNK_ROWS], F32)
+            for i in range(BANK_SLICES):
+                s = bank * BANK_SLICES + i
+                for o in range(OPERANDS):
+                    nc.tensor.matmul_mx(
+                        out=z[:, i, :],
+                        lhsT=w_codes[:, o, s * P * PACK : (s + 1) * P * PACK].bitcast(FP8X4),
+                        lhsT_scale=w_planes[:, o, s * P : (s + 1) * P],
+                        rhs=x_codes[:, o, cols].bitcast(FP8X4),
+                        rhs_scale=x_planes[:, o, cols],
+                        start=(o == 0),
+                        stop=(o == OPERANDS - 1),
+                    )
+            for i in range(BANK_SLICES):
+                s = bank * BANK_SLICES + i
+                nc.scalar.activation(
+                    out=att_t[:, s, :], in_=z[:, i, :], func=SIGMOID, bias=bias_cols[:, s : s + 1], scale=1.0
+                )
+
+        def difference(ch):
+            tiles = slice(ch * CHUNK, (ch + 1) * CHUNK)
+            nc.vector.tensor_tensor(
+                out=diff[:, tiles, :], in0=c_sb[:, tiles, :], in1=x_sb[STATE][:, tiles, :], op=SUB
+            )
+
+        def blend(ch, att_t):
+            for j in range(CHUNK):
+                t = ch * CHUNK + j
+                att = psum_a.tile([P, HID], F32)
+                for s in range(SLICES):
+                    nc.tensor.transpose(att[:, s * P : (s + 1) * P], att_t[:, s, j * P : (j + 1) * P], ident[:])
+                nc.vector.tensor_tensor(out=out_sb[:, t, :], in0=att[:], in1=diff[:, t, :], op=MULT)
+                nc.vector.tensor_tensor(out=out_sb[:, t, :], in0=out_sb[:, t, :], in1=x_sb[STATE][:, t, :], op=ADD)
+                nc.sync.dma_start(out=by_tile(out)[:, t, :], in_=out_sb[:, t, :])
+
+        att_ts = {}
+        for ch in range(-1, CHUNKS + 1):
+            ahead = ch + 1 < CHUNKS
+            now = 0 <= ch < CHUNKS
+            if now:
+                att_ts[ch] = work.tile([P, SLICES, CHUNK_ROWS], F32, name="att_t")
+            if ahead:
+                quantise(ch + 1, 0)
+                quantise(ch + 1, 1)
+            if now:
+                gate(ch, att_ts[ch], 0)
+            if ahead:
+                quantise(ch + 1, 2)
+                difference(ch + 1)
+            if ch == -1:
+                bias_to_partitions()
+            if ch >= 1:
+                blend(ch - 1, att_ts[ch - 1])
+            if now:
+                gate(ch, att_ts[ch], 1)

@@ -59,7 +59,6 @@ def tile_parentgru_pb_kernel(
         psum_x = ctx.enter_context(tc.psum_pool(name="psum_x", bufs=3))
         psum_z = ctx.enter_context(tc.psum_pool(name="psum_z", bufs=2))
         psum_a = ctx.enter_context(tc.psum_pool(name="psum_a", bufs=2))
-        ctx.enter_context(tc.manual_schedule())
 
         def by_tile(dram):
             return dram.rearrange("(p j) f -> p j f", j=TILES)

@@ -33,6 +33,11 @@ LIVE = 4
 FLOPS = 2 * BATCH * OPERANDS * K * HID
 
 
+ORDER = (1, 0, 2)
+WARM_START = 0
+WARM_HEAD = False
+
+
 def tile_parentgru_pb_kernel(
     tc,
     inputs,
@@ -59,6 +64,8 @@ def tile_parentgru_pb_kernel(
         psum_x = ctx.enter_context(tc.psum_pool(name="psum_x", bufs=3))
         psum_z = ctx.enter_context(tc.psum_pool(name="psum_z", bufs=2))
         psum_a = ctx.enter_context(tc.psum_pool(name="psum_a", bufs=2))
+        psum_w = ctx.enter_context(tc.psum_pool(name="psum_w", bufs=1))
+        ctx.enter_context(tc.manual_schedule())
 
         def by_tile(dram):
             return dram.rearrange("(p j) f -> p j f", j=TILES)
@@ -76,6 +83,7 @@ def tile_parentgru_pb_kernel(
         bias_rows_f32 = keep.tile([P, P], F32)
         bias_cols = keep.tile([P, SLICES], F32)
         warm = keep.tile([P, 1], F32)
+        scratch = psum_w.tile([P, P], F32)
 
         nc.vector.memset(w_planes[:].bitcast(I32), 0)
         nc.vector.memset(bias_rows[:], 0.0)
@@ -83,66 +91,81 @@ def tile_parentgru_pb_kernel(
         masks.make_identity(nc, ident[:])
         nc.scalar.activation(out=warm[:], in_=warm[:], func=SIGMOID)
 
-        def load_chunk(ch):
-            tiles = slice(ch * CHUNK, (ch + 1) * CHUNK)
-            for o in range(OPERANDS):
-                nc.sync.dma_start(out=x_sb[o][:, tiles, :], in_=by_tile(activations[o])[:, tiles, :])
-            nc.gpsimd.dma_start(out=c_sb[:, tiles, :], in_=by_tile(c)[:, tiles, :])
+        def tiles_of(ch):
+            return slice(ch * CHUNK, (ch + 1) * CHUNK)
 
-        load_chunk(0)
+        def load_x(ch, o):
+            nc.sync.dma_start(out=x_sb[o][:, tiles_of(ch), :], in_=by_tile(activations[o])[:, tiles_of(ch), :])
+
+        def load_c(ch):
+            nc.sync.dma_start(out=c_sb[:, tiles_of(ch), :], in_=by_tile(c)[:, tiles_of(ch), :])
+
+        load_x(0, ORDER[0])
         nc.sync.dma_start(out=bias_rows[0:SLICES, :], in_=w_a_b.rearrange("(s m) -> s m", m=P))
-        for o in range(OPERANDS):
+        load_x(0, ORDER[1])
+        load_x(0, ORDER[2])
+        for o in ORDER:
             for quad in range(P // QUADRANT):
                 nc.sync.dma_start(
                     out=w_planes[quad * QUADRANT : quad * QUADRANT + LIVE, o, :].bitcast(I32),
                     in_=weight_scales[o].bitcast(I32)[0, quad * LIVE : (quad + 1) * LIVE, :],
                 )
+        for o in ORDER:
             nc.sync.dma_start(
                 out=w_codes[:, o, :].bitcast(I32),
                 in_=weight_words[o][0].rearrange("p n t -> p (n t)").bitcast(I32),
             )
+        load_c(0)
         for ch in range(1, CHUNKS):
-            load_chunk(ch)
+            for o in ORDER:
+                load_x(ch, o)
+            load_c(ch)
 
-        def quantise(ch, o):
-            cols = slice(ch * CHUNK_ROWS, (ch + 1) * CHUNK_ROWS)
+        def dummy():
+            nc.tensor.matmul(out=scratch[:], lhsT=ident[:], rhs=ident[:], start=True, stop=True)
+
+        def transposes(ch, o):
             words = x_sb[o][:].bitcast(F32).rearrange("r j (p u) -> r j u p", u=2)
             xt = psum_x.tile([P, CHUNK, 2, P], F32, tag="xt")
             for j in range(CHUNK):
                 for u in range(2):
                     nc.tensor.transpose(xt[:, j, u, :], words[:, ch * CHUNK + j, u, :], ident[:])
+            return xt
+
+        def copy_out(xt):
             grouped = work.tile([P, CHUNK_ROWS * PACK], BF16, align_bytes=64)
             nc.scalar.copy(
                 out=grouped[:].bitcast(F32).rearrange("p (j r u) -> p j r u", j=CHUNK, u=2),
                 in_=xt[:].rearrange("p j u r -> p j r u"),
             )
+            return grouped
+
+        def quantise(ch, o, grouped):
+            cols = slice(ch * CHUNK_ROWS, (ch + 1) * CHUNK_ROWS)
             nc.vector.quantize_mx(
                 out=x_codes[:, o, cols].bitcast(FP8X4),
                 scales=x_planes[:, o, cols],
                 in_=grouped[:],
             )
 
-        def bias_to_partitions():
-            nc.vector.tensor_copy(out=bias_rows_f32[:], in_=bias_rows[:])
-            bias_t = psum_x.tile([P, P], F32, tag="xt")
-            nc.tensor.transpose(bias_t[:], bias_rows_f32[:], ident[:])
-            nc.vector.tensor_copy(out=bias_cols[:], in_=bias_t[:, 0:SLICES])
-
-        def gate(ch, att_t, bank):
+        def passes(ch, bank):
             cols = slice(ch * CHUNK_ROWS, (ch + 1) * CHUNK_ROWS)
             z = psum_z.tile([P, BANK_SLICES, CHUNK_ROWS], F32)
             for i in range(BANK_SLICES):
                 s = bank * BANK_SLICES + i
-                for o in range(OPERANDS):
+                for n, o in enumerate(ORDER):
                     nc.tensor.matmul_mx(
                         out=z[:, i, :],
                         lhsT=w_codes[:, o, s * P * PACK : (s + 1) * P * PACK].bitcast(FP8X4),
                         lhsT_scale=w_planes[:, o, s * P : (s + 1) * P],
                         rhs=x_codes[:, o, cols].bitcast(FP8X4),
                         rhs_scale=x_planes[:, o, cols],
-                        start=(o == 0),
-                        stop=(o == OPERANDS - 1),
+                        start=(n == 0),
+                        stop=(n == OPERANDS - 1),
                     )
+            return z
+
+        def sigmoids(bank, z, att_t):
             for i in range(BANK_SLICES):
                 s = bank * BANK_SLICES + i
                 nc.scalar.activation(
@@ -150,38 +173,83 @@ def tile_parentgru_pb_kernel(
                 )
 
         def difference(ch):
-            tiles = slice(ch * CHUNK, (ch + 1) * CHUNK)
             nc.vector.tensor_tensor(
-                out=diff[:, tiles, :], in0=c_sb[:, tiles, :], in1=x_sb[STATE][:, tiles, :], op=SUB
+                out=diff[:, tiles_of(ch), :], in0=c_sb[:, tiles_of(ch), :], in1=x_sb[STATE][:, tiles_of(ch), :], op=SUB
             )
 
-        def blend(ch, att_t):
-            for j in range(CHUNK):
-                t = ch * CHUNK + j
-                att = psum_a.tile([P, HID], F32)
-                for s in range(SLICES):
-                    nc.tensor.transpose(att[:, s * P : (s + 1) * P], att_t[:, s, j * P : (j + 1) * P], ident[:])
-                nc.vector.tensor_tensor(out=out_sb[:, t, :], in0=att[:], in1=diff[:, t, :], op=MULT)
-                nc.vector.tensor_tensor(out=out_sb[:, t, :], in0=out_sb[:, t, :], in1=x_sb[STATE][:, t, :], op=ADD)
-                nc.sync.dma_start(out=by_tile(out)[:, t, :], in_=out_sb[:, t, :])
+        def back(j, att_t):
+            att = psum_a.tile([P, HID], F32)
+            for s in range(SLICES):
+                nc.tensor.transpose(att[:, s * P : (s + 1) * P], att_t[:, s, j * P : (j + 1) * P], ident[:])
+            return att
+
+        def mult(t, att):
+            nc.vector.tensor_tensor(out=out_sb[:, t, :], in0=att[:], in1=diff[:, t, :], op=MULT)
+
+        def add_store(tiles):
+            nc.vector.tensor_tensor(
+                out=out_sb[:, tiles, :], in0=out_sb[:, tiles, :], in1=x_sb[STATE][:, tiles, :], op=ADD
+            )
+            nc.sync.dma_start(out=by_tile(out)[:, tiles, :], in_=out_sb[:, tiles, :])
 
         att_ts = {}
-        for ch in range(-1, CHUNKS + 1):
-            ahead = ch + 1 < CHUNKS
-            now = 0 <= ch < CHUNKS
-            if now:
+
+        def gate(ch, bank):
+            if bank == 0:
                 att_ts[ch] = work.tile([P, SLICES, CHUNK_ROWS], F32, name="att_t")
+            sigmoids(bank, passes(ch, bank), att_ts[ch])
+
+        def blend_products(ch):
+            atts = [back(j, att_ts[ch]) for j in range(CHUNK)]
+            for j in range(CHUNK):
+                mult(ch * CHUNK + j, atts[j])
+
+        for n in range(WARM_START):
+            dummy()
+        nc.vector.tensor_copy(out=bias_rows_f32[:], in_=bias_rows[:])
+        for n, o in enumerate(ORDER):
+            xt = transposes(0, o)
+            if n == 0:
+                bias_t = psum_x.tile([P, P], F32, tag="xt")
+                nc.tensor.transpose(bias_t[:], bias_rows_f32[:], ident[:])
+            if WARM_HEAD:
+                dummy()
+            quantise(0, o, copy_out(xt))
+            if n == 0:
+                nc.vector.tensor_copy(out=bias_cols[:], in_=bias_t[:, 0:SLICES])
+        if WARM_HEAD:
+            dummy()
+        difference(0)
+        gate(0, 0)
+        gate(0, 1)
+        for n, o in enumerate(ORDER):
+            xt = transposes(1, o)
+            if WARM_HEAD:
+                dummy()
+            quantise(1, o, copy_out(xt))
+        difference(1)
+
+        for ch in range(1, CHUNKS):
+            ahead = ch + 1 < CHUNKS
             if ahead:
-                quantise(ch + 1, 0)
-                quantise(ch + 1, 1)
-            if now:
-                gate(ch, att_ts[ch], 0)
+                first = copy_out(transposes(ch + 1, ORDER[0]))
+            else:
+                gate(ch, 0)
+            blend_products(ch - 1)
             if ahead:
-                quantise(ch + 1, 2)
+                quantise(ch + 1, ORDER[0], first)
+                gate(ch, 0)
+            add_store(tiles_of(ch - 1))
+            if ahead:
+                xts = [transposes(ch + 1, o) for o in ORDER[1:]]
+                groupeds = [copy_out(xt) for xt in xts]
+                for o, grouped in zip(ORDER[1:], groupeds):
+                    quantise(ch + 1, o, grouped)
                 difference(ch + 1)
-            if ch == -1:
-                bias_to_partitions()
-            if ch >= 1:
-                blend(ch - 1, att_ts[ch - 1])
-            if now:
-                gate(ch, att_ts[ch], 1)
+            gate(ch, 1)
+
+        last = CHUNKS - 1
+        blend_products(last)
+        for j in range(CHUNK):
+            t = last * CHUNK + j
+            add_store(slice(t, t + 1))

@@ -34,8 +34,7 @@ FLOPS = 2 * BATCH * OPERANDS * K * HID
 
 
 ORDER = (1, 0, 2)
-WARM_START = 0
-WARM_HEAD = False
+LEAD = 2
 
 
 def tile_parentgru_pb_kernel(
@@ -64,7 +63,6 @@ def tile_parentgru_pb_kernel(
         psum_x = ctx.enter_context(tc.psum_pool(name="psum_x", bufs=3))
         psum_z = ctx.enter_context(tc.psum_pool(name="psum_z", bufs=2))
         psum_a = ctx.enter_context(tc.psum_pool(name="psum_a", bufs=2))
-        psum_w = ctx.enter_context(tc.psum_pool(name="psum_w", bufs=1))
         ctx.enter_context(tc.manual_schedule())
 
         def by_tile(dram):
@@ -79,17 +77,15 @@ def tile_parentgru_pb_kernel(
         diff = keep.tile([P, TILES, HID], F32)
         out_sb = keep.tile([P, TILES, HID], F32)
         ident = keep.tile([P, P], F32)
-        bias_rows = keep.tile([P, P], BF16)
-        bias_rows_f32 = keep.tile([P, P], F32)
-        bias_cols = keep.tile([P, SLICES], F32)
+        bias_cols = keep.tile([P, SLICES, 2], BF16)
         warm = keep.tile([P, 1], F32)
-        scratch = psum_w.tile([P, P], F32)
 
         nc.vector.memset(w_planes[:].bitcast(I32), 0)
-        nc.vector.memset(bias_rows[:], 0.0)
         nc.vector.memset(warm[:], 0.0)
         masks.make_identity(nc, ident[:])
         nc.scalar.activation(out=warm[:], in_=warm[:], func=SIGMOID)
+        with nc.allow_non_contiguous_dma(reason="512 bias values, one to a partition and slice"):
+            nc.gpsimd.dma_start(out=bias_cols[:, :, 0], in_=w_a_b.rearrange("(s m) -> m s", m=P))
 
         def tiles_of(ch):
             return slice(ch * CHUNK, (ch + 1) * CHUNK)
@@ -100,29 +96,31 @@ def tile_parentgru_pb_kernel(
         def load_c(ch):
             nc.sync.dma_start(out=c_sb[:, tiles_of(ch), :], in_=by_tile(c)[:, tiles_of(ch), :])
 
-        load_x(0, ORDER[0])
-        nc.sync.dma_start(out=bias_rows[0:SLICES, :], in_=w_a_b.rearrange("(s m) -> s m", m=P))
-        load_x(0, ORDER[1])
-        load_x(0, ORDER[2])
-        for o in ORDER:
-            for quad in range(P // QUADRANT):
-                nc.sync.dma_start(
-                    out=w_planes[quad * QUADRANT : quad * QUADRANT + LIVE, o, :].bitcast(I32),
-                    in_=weight_scales[o].bitcast(I32)[0, quad * LIVE : (quad + 1) * LIVE, :],
-                )
-        for o in ORDER:
+        def load_codes(o):
             nc.sync.dma_start(
                 out=w_codes[:, o, :].bitcast(I32),
                 in_=weight_words[o][0].rearrange("p n t -> p (n t)").bitcast(I32),
             )
-        load_c(0)
-        for ch in range(1, CHUNKS):
-            for o in ORDER:
-                load_x(ch, o)
-            load_c(ch)
 
-        def dummy():
-            nc.tensor.matmul(out=scratch[:], lhsT=ident[:], rhs=ident[:], start=True, stop=True)
+        def load_scale_rows(o, quad):
+            nc.sync.dma_start(
+                out=w_planes[quad * QUADRANT : quad * QUADRANT + LIVE, o, :].bitcast(I32),
+                in_=weight_scales[o].bitcast(I32)[0, quad * LIVE : (quad + 1) * LIVE, :],
+            )
+
+        def chunk_loads(ch):
+            return [(load_x, (ch, ORDER[0])), (load_c, (ch,)), (load_x, (ch, ORDER[1])), (load_x, (ch, ORDER[2]))]
+
+        big = chunk_loads(0) + chunk_loads(1) + [(load_codes, (o,)) for o in ORDER]
+        small = [(o, quad) for o in ORDER for quad in range(P // QUADRANT)]
+        for n, (load, args) in enumerate(big):
+            load(*args)
+            load_scale_rows(*small[n])
+        for rest in small[len(big) :]:
+            load_scale_rows(*rest)
+        for ch in range(LEAD, CHUNKS):
+            for load, args in chunk_loads(ch):
+                load(*args)
 
         def transposes(ch, o):
             words = x_sb[o][:].bitcast(F32).rearrange("r j (p u) -> r j u p", u=2)
@@ -169,7 +167,7 @@ def tile_parentgru_pb_kernel(
             for i in range(BANK_SLICES):
                 s = bank * BANK_SLICES + i
                 nc.scalar.activation(
-                    out=att_t[:, s, :], in_=z[:, i, :], func=SIGMOID, bias=bias_cols[:, s : s + 1], scale=1.0
+                    out=att_t[:, s, :], in_=z[:, i, :], func=SIGMOID, bias=bias_cols[:, s, 0:1], scale=1.0
                 )
 
         def difference(ch):
@@ -192,6 +190,11 @@ def tile_parentgru_pb_kernel(
             )
             nc.sync.dma_start(out=by_tile(out)[:, tiles, :], in_=out_sb[:, tiles, :])
 
+        def add_store_by_tile(ch):
+            for j in range(CHUNK):
+                t = ch * CHUNK + j
+                add_store(slice(t, t + 1))
+
         att_ts = {}
 
         def gate(ch, bank):
@@ -204,52 +207,34 @@ def tile_parentgru_pb_kernel(
             for j in range(CHUNK):
                 mult(ch * CHUNK + j, atts[j])
 
-        for n in range(WARM_START):
-            dummy()
-        nc.vector.tensor_copy(out=bias_rows_f32[:], in_=bias_rows[:])
-        for n, o in enumerate(ORDER):
-            xt = transposes(0, o)
-            if n == 0:
-                bias_t = psum_x.tile([P, P], F32, tag="xt")
-                nc.tensor.transpose(bias_t[:], bias_rows_f32[:], ident[:])
-            if WARM_HEAD:
-                dummy()
-            quantise(0, o, copy_out(xt))
-            if n == 0:
-                nc.vector.tensor_copy(out=bias_cols[:], in_=bias_t[:, 0:SLICES])
-        if WARM_HEAD:
-            dummy()
-        difference(0)
-        gate(0, 0)
-        gate(0, 1)
-        for n, o in enumerate(ORDER):
-            xt = transposes(1, o)
-            if WARM_HEAD:
-                dummy()
-            quantise(1, o, copy_out(xt))
-        difference(1)
+        for ch in range(LEAD):
+            difference(ch)
+            for o in ORDER:
+                quantise(ch, o, copy_out(transposes(ch, o)))
 
-        for ch in range(1, CHUNKS):
-            ahead = ch + 1 < CHUNKS
+        for ch in range(CHUNKS):
+            ahead = ch + LEAD < CHUNKS
+            gate(ch, 0)
             if ahead:
-                first = copy_out(transposes(ch + 1, ORDER[0]))
-            else:
-                gate(ch, 0)
-            blend_products(ch - 1)
+                first = copy_out(transposes(ch + LEAD, ORDER[0]))
+            if ch >= 1:
+                blend_products(ch - 1)
+            if ch == 0:
+                difference(LEAD)
             if ahead:
-                quantise(ch + 1, ORDER[0], first)
-                gate(ch, 0)
-            add_store(tiles_of(ch - 1))
+                quantise(ch + LEAD, ORDER[0], first)
+            if ch == 0:
+                difference(LEAD + 1)
+            if ch == 1:
+                add_store(tiles_of(0))
+            if ch > 1:
+                add_store_by_tile(ch - 1)
+            gate(ch, 1)
             if ahead:
-                xts = [transposes(ch + 1, o) for o in ORDER[1:]]
+                xts = [transposes(ch + LEAD, o) for o in ORDER[1:]]
                 groupeds = [copy_out(xt) for xt in xts]
                 for o, grouped in zip(ORDER[1:], groupeds):
-                    quantise(ch + 1, o, grouped)
-                difference(ch + 1)
-            gate(ch, 1)
+                    quantise(ch + LEAD, o, grouped)
 
-        last = CHUNKS - 1
-        blend_products(last)
-        for j in range(CHUNK):
-            t = last * CHUNK + j
-            add_store(slice(t, t + 1))
+        blend_products(CHUNKS - 1)
+        add_store_by_tile(CHUNKS - 1)

@@ -77,15 +77,17 @@ def tile_parentgru_pb_kernel(
         diff = keep.tile([P, TILES, HID], F32)
         out_sb = keep.tile([P, TILES, HID], F32)
         ident = keep.tile([P, P], F32)
-        bias_cols = keep.tile([P, SLICES, 2], BF16)
+        bias_rows = keep.tile([P, P], BF16)
+        bias_rows_f32 = keep.tile([P, P], F32)
+        bias_cols = keep.tile([P, SLICES], F32)
         warm = keep.tile([P, 1], F32)
 
         nc.vector.memset(w_planes[:].bitcast(I32), 0)
         nc.vector.memset(warm[:], 0.0)
+        nc.vector.memset(bias_rows[:], 0.0)
         masks.make_identity(nc, ident[:])
         nc.scalar.activation(out=warm[:], in_=warm[:], func=SIGMOID)
-        with nc.allow_non_contiguous_dma(reason="512 bias values, one to a partition and slice"):
-            nc.gpsimd.dma_start(out=bias_cols[:, :, 0], in_=w_a_b.rearrange("(s m) -> m s", m=P))
+        nc.gpsimd.dma_start(out=bias_rows[0:SLICES, :], in_=w_a_b.rearrange("(s m) -> s m", m=P))
 
         def tiles_of(ch):
             return slice(ch * CHUNK, (ch + 1) * CHUNK)
@@ -167,7 +169,7 @@ def tile_parentgru_pb_kernel(
             for i in range(BANK_SLICES):
                 s = bank * BANK_SLICES + i
                 nc.scalar.activation(
-                    out=att_t[:, s, :], in_=z[:, i, :], func=SIGMOID, bias=bias_cols[:, s, 0:1], scale=1.0
+                    out=att_t[:, s, :], in_=z[:, i, :], func=SIGMOID, bias=bias_cols[:, s : s + 1], scale=1.0
                 )
 
         def difference(ch):
@@ -209,8 +211,14 @@ def tile_parentgru_pb_kernel(
 
         for ch in range(LEAD):
             difference(ch)
+            if ch == 0:
+                nc.vector.tensor_copy(out=bias_rows_f32[:], in_=bias_rows[:])
             for o in ORDER:
                 quantise(ch, o, copy_out(transposes(ch, o)))
+            if ch == 0:
+                bias_t = psum_x.tile([P, P], F32, tag="xt")
+                nc.tensor.transpose(bias_t[:], bias_rows_f32[:], ident[:])
+                nc.vector.tensor_copy(out=bias_cols[:], in_=bias_t[:, 0:SLICES])
 
         for ch in range(CHUNKS):
             ahead = ch + LEAD < CHUNKS

@@ -63,6 +63,7 @@ def tile_parentgru_pb_kernel(
         psum_x = ctx.enter_context(tc.psum_pool(name="psum_x", bufs=3))
         psum_z = ctx.enter_context(tc.psum_pool(name="psum_z", bufs=2))
         psum_a = ctx.enter_context(tc.psum_pool(name="psum_a", bufs=2))
+        psum_w = ctx.enter_context(tc.psum_pool(name="psum_w", bufs=1))
         ctx.enter_context(tc.manual_schedule())
 
         def by_tile(dram):
@@ -81,6 +82,7 @@ def tile_parentgru_pb_kernel(
         bias_rows_f32 = keep.tile([P, P], F32)
         bias_cols = keep.tile([P, SLICES], F32)
         warm = keep.tile([P, 1], F32)
+        scratch = psum_w.tile([P, P], F32)
 
         nc.vector.memset(w_planes[:].bitcast(I32), 0)
         nc.vector.memset(warm[:], 0.0)
@@ -209,16 +211,26 @@ def tile_parentgru_pb_kernel(
             for j in range(CHUNK):
                 mult(ch * CHUNK + j, atts[j])
 
+        def dummy():
+            nc.tensor.matmul(out=scratch[:], lhsT=ident[:], rhs=ident[:], start=True, stop=True)
+
+        for n in range(3):
+            dummy()
         for ch in range(LEAD):
             difference(ch)
             if ch == 0:
                 nc.vector.tensor_copy(out=bias_rows_f32[:], in_=bias_rows[:])
             for o in ORDER:
-                quantise(ch, o, copy_out(transposes(ch, o)))
+                xt = transposes(ch, o)
+                dummy()
+                quantise(ch, o, copy_out(xt))
             if ch == 0:
                 bias_t = psum_x.tile([P, P], F32, tag="xt")
                 nc.tensor.transpose(bias_t[:], bias_rows_f32[:], ident[:])
                 nc.vector.tensor_copy(out=bias_cols[:], in_=bias_t[:, 0:SLICES])
+
+        dummy()
+        dummy()
 
         for ch in range(CHUNKS):
             ahead = ch + LEAD < CHUNKS

@@ -61,9 +61,8 @@ def tile_parentgru_pb_kernel(
         keep = ctx.enter_context(tc.tile_pool(name="keep", bufs=1))
         work = ctx.enter_context(tc.tile_pool(name="work", bufs=3))
         psum_x = ctx.enter_context(tc.psum_pool(name="psum_x", bufs=3))
-        psum_z = ctx.enter_context(tc.psum_pool(name="psum_z", bufs=2))
+        psum_z = ctx.enter_context(tc.psum_pool(name="psum_z", bufs=3))
         psum_a = ctx.enter_context(tc.psum_pool(name="psum_a", bufs=2))
-        psum_w = ctx.enter_context(tc.psum_pool(name="psum_w", bufs=1))
         ctx.enter_context(tc.manual_schedule())
 
         def by_tile(dram):
@@ -82,7 +81,7 @@ def tile_parentgru_pb_kernel(
         bias_rows_f32 = keep.tile([P, P], F32)
         bias_cols = keep.tile([P, SLICES], F32)
         warm = keep.tile([P, 1], F32)
-        scratch = psum_w.tile([P, P], F32)
+        scratch = psum_z.tile([P, P], F32, tag="z")
 
         nc.vector.memset(w_planes[:].bitcast(I32), 0)
         nc.vector.memset(warm[:], 0.0)
@@ -150,29 +149,25 @@ def tile_parentgru_pb_kernel(
                 in_=grouped[:],
             )
 
-        def passes(ch, bank):
+        def passes(ch, s):
             cols = slice(ch * CHUNK_ROWS, (ch + 1) * CHUNK_ROWS)
-            z = psum_z.tile([P, BANK_SLICES, CHUNK_ROWS], F32)
-            for i in range(BANK_SLICES):
-                s = bank * BANK_SLICES + i
-                for n, o in enumerate(ORDER):
-                    nc.tensor.matmul_mx(
-                        out=z[:, i, :],
-                        lhsT=w_codes[:, o, s * P * PACK : (s + 1) * P * PACK].bitcast(FP8X4),
-                        lhsT_scale=w_planes[:, o, s * P : (s + 1) * P],
-                        rhs=x_codes[:, o, cols].bitcast(FP8X4),
-                        rhs_scale=x_planes[:, o, cols],
-                        start=(n == 0),
-                        stop=(n == OPERANDS - 1),
-                    )
+            z = psum_z.tile([P, CHUNK_ROWS], F32, tag="z")
+            for n, o in enumerate(ORDER):
+                nc.tensor.matmul_mx(
+                    out=z[:],
+                    lhsT=w_codes[:, o, s * P * PACK : (s + 1) * P * PACK].bitcast(FP8X4),
+                    lhsT_scale=w_planes[:, o, s * P : (s + 1) * P],
+                    rhs=x_codes[:, o, cols].bitcast(FP8X4),
+                    rhs_scale=x_planes[:, o, cols],
+                    start=(n == 0),
+                    stop=(n == OPERANDS - 1),
+                )
             return z
 
-        def sigmoids(bank, z, att_t):
-            for i in range(BANK_SLICES):
-                s = bank * BANK_SLICES + i
-                nc.scalar.activation(
-                    out=att_t[:, s, :], in_=z[:, i, :], func=SIGMOID, bias=bias_cols[:, s : s + 1], scale=1.0
-                )
+        def sigmoid(s, z, att_t, cols=slice(0, CHUNK_ROWS)):
+            nc.scalar.activation(
+                out=att_t[:, s, cols], in_=z[:, cols], func=SIGMOID, bias=bias_cols[:, s : s + 1], scale=1.0
+            )
 
         def difference(ch):
             nc.vector.tensor_tensor(
@@ -204,7 +199,13 @@ def tile_parentgru_pb_kernel(
         def gate(ch, bank):
             if bank == 0:
                 att_ts[ch] = work.tile([P, SLICES, CHUNK_ROWS], F32, name="att_t")
-            sigmoids(bank, passes(ch, bank), att_ts[ch])
+            for s in range(bank * BANK_SLICES, (bank + 1) * BANK_SLICES):
+                z = passes(ch, s)
+                if ch == CHUNKS - 1 and s == SLICES - 1:
+                    for j in range(CHUNK):
+                        sigmoid(s, z, att_ts[ch], slice(j * P, (j + 1) * P))
+                else:
+                    sigmoid(s, z, att_ts[ch])
 
         def blend_products(ch):
             atts = [back(j, att_ts[ch]) for j in range(CHUNK)]
@@ -257,4 +258,10 @@ def tile_parentgru_pb_kernel(
                     quantise(ch + LEAD, o, grouped)
 
         blend_products(CHUNKS - 1)
-        add_store_by_tile(CHUNKS - 1)
+        add_store(slice(TILES - 2, TILES - 1))
+        for half in range(2):
+            cols = slice(half * HID // 2, (half + 1) * HID // 2)
+            nc.vector.tensor_tensor(
+                out=out_sb[:, TILES - 1, cols], in0=out_sb[:, TILES - 1, cols], in1=x_sb[STATE][:, TILES - 1, cols], op=ADD
+            )
+            nc.sync.dma_start(out=by_tile(out)[:, TILES - 1, cols], in_=out_sb[:, TILES - 1, cols])

from contextlib import ExitStack

import concourse.masks as masks
import concourse.mybir as mybir

F32 = mybir.dt.float32
BF16 = mybir.dt.bfloat16
I32 = mybir.dt.int32
U32 = mybir.dt.uint32
U8 = mybir.dt.uint8
FP8X4 = mybir.dt.float8_e4m3fn_x4
ADD = mybir.AluOpType.add
SUB = mybir.AluOpType.subtract
MULT = mybir.AluOpType.mult
SIGMOID = mybir.ActivationFunctionType.Sigmoid

P = 128
PACK = 4
BATCH = 1024
K = 512
HID = 512
OPERANDS = 3
STATE = 1
TILES = BATCH // P
CHUNK = 2
CHUNKS = TILES // CHUNK
CHUNK_ROWS = CHUNK * P
SLICES = HID // P
BANK_SLICES = 2
QUADRANT = 32
LIVE = 4

FLOPS = 2 * BATCH * OPERANDS * K * HID


ORDER = (1, 0, 2)
LEAD = 2


def tile_parentgru_pb_kernel(
    tc,
    inputs,
    state,
    parent_state,
    c,
    w_a_w_words,
    w_a_w_scales,
    w_a_b,
    u_a_w_words,
    u_a_w_scales,
    p_a_w_words,
    p_a_w_scales,
    out,
):
    nc = tc.nc
    activations = (inputs, state, parent_state)
    weight_words = (w_a_w_words, u_a_w_words, p_a_w_words)
    weight_scales = (w_a_w_scales, u_a_w_scales, p_a_w_scales)

    with ExitStack() as ctx:
        keep = ctx.enter_context(tc.tile_pool(name="keep", bufs=1))
        work = ctx.enter_context(tc.tile_pool(name="work", bufs=3))
        psum_x = ctx.enter_context(tc.psum_pool(name="psum_x", bufs=3))
        psum_z = ctx.enter_context(tc.psum_pool(name="psum_z", bufs=3))
        psum_a = ctx.enter_context(tc.psum_pool(name="psum_a", bufs=2))
        ctx.enter_context(tc.manual_schedule())

        def by_tile(dram):
            return dram.rearrange("(p j) f -> p j f", j=TILES)

        x_sb = [keep.tile([P, TILES, K], BF16, name="x_sb%d" % o) for o in range(OPERANDS)]
        c_sb = keep.tile([P, TILES, HID], BF16)
        w_codes = keep.tile([P, OPERANDS, HID * PACK], U8, align_bytes=64)
        w_planes = keep.tile([P, OPERANDS, HID], U8, align_bytes=64)
        x_codes = keep.tile([P, OPERANDS, BATCH], U32, align_bytes=64)
        x_planes = keep.tile([P, OPERANDS, BATCH], U8, align_bytes=64)
        diff = keep.tile([P, TILES, HID], F32)
        out_sb = keep.tile([P, TILES, HID], F32)
        ident = keep.tile([P, P], F32)
        bias_rows = keep.tile([P, P], BF16)
        bias_rows_f32 = keep.tile([P, P], F32)
        bias_cols = keep.tile([P, SLICES], F32)
        warm = keep.tile([P, 1], F32)
        scratch = psum_z.tile([P, P], F32, tag="z")

        nc.vector.memset(w_planes[:].bitcast(I32), 0)
        nc.vector.memset(warm[:], 0.0)
        nc.vector.memset(bias_rows[:], 0.0)
        masks.make_identity(nc, ident[:])
        nc.scalar.activation(out=warm[:], in_=warm[:], func=SIGMOID)
        nc.gpsimd.dma_start(out=bias_rows[0:SLICES, :], in_=w_a_b.rearrange("(s m) -> s m", m=P))

        def tiles_of(ch):
            return slice(ch * CHUNK, (ch + 1) * CHUNK)

        def load_x(ch, o):
            nc.sync.dma_start(out=x_sb[o][:, tiles_of(ch), :], in_=by_tile(activations[o])[:, tiles_of(ch), :])

        def load_c(ch):
            nc.sync.dma_start(out=c_sb[:, tiles_of(ch), :], in_=by_tile(c)[:, tiles_of(ch), :])

        def load_codes(o):
            nc.sync.dma_start(
                out=w_codes[:, o, :].bitcast(I32),
                in_=weight_words[o][0].rearrange("p n t -> p (n t)").bitcast(I32),
            )

        def load_scale_rows(o, quad):
            nc.sync.dma_start(
                out=w_planes[quad * QUADRANT : quad * QUADRANT + LIVE, o, :].bitcast(I32),
                in_=weight_scales[o].bitcast(I32)[0, quad * LIVE : (quad + 1) * LIVE, :],
            )

        def chunk_loads(ch):
            return [(load_x, (ch, ORDER[0])), (load_c, (ch,)), (load_x, (ch, ORDER[1])), (load_x, (ch, ORDER[2]))]

        big = chunk_loads(0) + chunk_loads(1) + [(load_codes, (o,)) for o in ORDER]
        small = [(o, quad) for o in ORDER for quad in range(P // QUADRANT)]
        for n, (load, args) in enumerate(big):
            load(*args)
            load_scale_rows(*small[n])
        for rest in small[len(big) :]:
            load_scale_rows(*rest)
        for ch in range(LEAD, CHUNKS):
            for load, args in chunk_loads(ch):
                load(*args)

        def transposes(ch, o):
            words = x_sb[o][:].bitcast(F32).rearrange("r j (p u) -> r j u p", u=2)
            xt = psum_x.tile([P, CHUNK, 2, P], F32, tag="xt")
            for j in range(CHUNK):
                for u in range(2):
                    nc.tensor.transpose(xt[:, j, u, :], words[:, ch * CHUNK + j, u, :], ident[:])
            return xt

        def copy_out(xt):
            grouped = work.tile([P, CHUNK_ROWS * PACK], BF16, align_bytes=64)
            nc.scalar.copy(
                out=grouped[:].bitcast(F32).rearrange("p (j r u) -> p j r u", j=CHUNK, u=2),
                in_=xt[:].rearrange("p j u r -> p j r u"),
            )
            return grouped

        def quantise(ch, o, grouped):
            cols = slice(ch * CHUNK_ROWS, (ch + 1) * CHUNK_ROWS)
            nc.vector.quantize_mx(
                out=x_codes[:, o, cols].bitcast(FP8X4),
                scales=x_planes[:, o, cols],
                in_=grouped[:],
            )

        def passes(ch, s):
            cols = slice(ch * CHUNK_ROWS, (ch + 1) * CHUNK_ROWS)
            z = psum_z.tile([P, CHUNK_ROWS], F32, tag="z")
            for n, o in enumerate(ORDER):
                nc.tensor.matmul_mx(
                    out=z[:],
                    lhsT=w_codes[:, o, s * P * PACK : (s + 1) * P * PACK].bitcast(FP8X4),
                    lhsT_scale=w_planes[:, o, s * P : (s + 1) * P],
                    rhs=x_codes[:, o, cols].bitcast(FP8X4),
                    rhs_scale=x_planes[:, o, cols],
                    start=(n == 0),
                    stop=(n == OPERANDS - 1),
                )
            return z

        def sigmoid(s, z, att_t, cols=slice(0, CHUNK_ROWS)):
            nc.scalar.activation(
                out=att_t[:, s, cols], in_=z[:, cols], func=SIGMOID, bias=bias_cols[:, s : s + 1], scale=1.0
            )

        def difference(ch):
            nc.vector.tensor_tensor(
                out=diff[:, tiles_of(ch), :], in0=c_sb[:, tiles_of(ch), :], in1=x_sb[STATE][:, tiles_of(ch), :], op=SUB
            )

        def back(j, att_t):
            att = psum_a.tile([P, HID], F32)
            for s in range(SLICES):
                nc.tensor.transpose(att[:, s * P : (s + 1) * P], att_t[:, s, j * P : (j + 1) * P], ident[:])
            return att

        def mult(t, att):
            nc.vector.tensor_tensor(out=out_sb[:, t, :], in0=att[:], in1=diff[:, t, :], op=MULT)

        def add_store(tiles):
            nc.vector.tensor_tensor(
                out=out_sb[:, tiles, :], in0=out_sb[:, tiles, :], in1=x_sb[STATE][:, tiles, :], op=ADD
            )
            nc.sync.dma_start(out=by_tile(out)[:, tiles, :], in_=out_sb[:, tiles, :])

        def add_store_by_tile(ch):
            for j in range(CHUNK):
                t = ch * CHUNK + j
                add_store(slice(t, t + 1))

        att_ts = {}

        def gate(ch, bank):
            if bank == 0:
                att_ts[ch] = work.tile([P, SLICES, CHUNK_ROWS], F32, name="att_t")
            for s in range(bank * BANK_SLICES, (bank + 1) * BANK_SLICES):
                z = passes(ch, s)
                if ch == CHUNKS - 1 and s == SLICES - 1:
                    for j in range(CHUNK):
                        sigmoid(s, z, att_ts[ch], slice(j * P, (j + 1) * P))
                else:
                    sigmoid(s, z, att_ts[ch])

        def blend_products(ch):
            atts = [back(j, att_ts[ch]) for j in range(CHUNK)]
            for j in range(CHUNK):
                mult(ch * CHUNK + j, atts[j])

        def dummy():
            nc.tensor.matmul(out=scratch[:], lhsT=ident[:], rhs=ident[:], start=True, stop=True)

        for n in range(3):
            dummy()
        for ch in range(LEAD):
            difference(ch)
            if ch == 0:
                nc.vector.tensor_copy(out=bias_rows_f32[:], in_=bias_rows[:])
            for o in ORDER:
                xt = transposes(ch, o)
                dummy()
                quantise(ch, o, copy_out(xt))
            if ch == 0:
                bias_t = psum_x.tile([P, P], F32, tag="xt")
                nc.tensor.transpose(bias_t[:], bias_rows_f32[:], ident[:])
                nc.vector.tensor_copy(out=bias_cols[:], in_=bias_t[:, 0:SLICES])

        dummy()
        dummy()

        for ch in range(CHUNKS):
            ahead = ch + LEAD < CHUNKS
            gate(ch, 0)
            if ahead:
                first = copy_out(transposes(ch + LEAD, ORDER[0]))
            if ch >= 1:
                blend_products(ch - 1)
            if ch == 0:
                difference(LEAD)
            if ahead:
                quantise(ch + LEAD, ORDER[0], first)
            if ch == 0:
                difference(LEAD + 1)
            if ch == 1:
                add_store(tiles_of(0))
            if ch > 1:
                add_store_by_tile(ch - 1)
            gate(ch, 1)
            if ahead:
                xts = [transposes(ch + LEAD, o) for o in ORDER[1:]]
                groupeds = [copy_out(xt) for xt in xts]
                for o, grouped in zip(ORDER[1:], groupeds):
                    quantise(ch + LEAD, o, grouped)

        blend_products(CHUNKS - 1)
        add_store(slice(TILES - 2, TILES - 1))
        for half in range(2):
            cols = slice(half * HID // 2, (half + 1) * HID // 2)
            nc.vector.tensor_tensor(
                out=out_sb[:, TILES - 1, cols], in0=out_sb[:, TILES - 1, cols], in1=x_sb[STATE][:, TILES - 1, cols], op=ADD
            )
            nc.sync.dma_start(out=by_tile(out)[:, TILES - 1, cols], in_=out_sb[:, TILES - 1, cols])
